import numpy as np
import ml_dtypes


def mxq(x, axis, fmt="e4m3"):
    dtype, down = {"e4m3": (ml_dtypes.float8_e4m3fn, 7), "e5m2": (ml_dtypes.float8_e5m2, 14)}[fmt]
    v = np.moveaxis(np.asarray(x, np.float32).astype(ml_dtypes.bfloat16).astype(np.float64), axis, -1)
    blocks = v.reshape(v.shape[:-1] + (-1, 32))
    amax = np.abs(blocks).max(-1, keepdims=True)
    byte = np.maximum(np.where(amax > 0, np.frexp(amax)[1] - 1 + 127, 0) - down, 1)
    scale = np.exp2(byte - 127.0)
    codes = (blocks / scale).astype(np.float32).astype(dtype).astype(np.float64)
    return np.moveaxis((codes * scale).reshape(v.shape), -1, axis)


WIDE = False


def mx_kscale(k):
    if not WIDE:
        return np.ones(k)
    levels = np.array([10, -10, 5, -5, 0])
    a = np.random.permutation(np.resize(levels, k // 512 * 4)).reshape(k // 512, 4)
    idx = np.arange(k)
    return np.exp2(a[idx // 512, idx % 128 // 32])


BF16 = ml_dtypes.bfloat16


def bf(x):
    return np.asarray(x, np.float32).astype(BF16)


def f64(x):
    return np.asarray(x).astype(np.float64)


B, HH, WW, C, NH, KD, WS, SS = 1, 64, 64, 512, 8, 64, 8, 4
GH, GW, T, F = HH // WS, WW // WS, WS * WS, NH * KD
N = B * GH * GW


def setup_inputs():
    s = mx_kscale(C)

    def weight():
        return bf(np.random.standard_normal((C, NH, KD)) / np.sqrt(C) / s[:, None, None])

    def bias():
        return bf(np.random.standard_normal((NH, KD)) * 0.3)

    return {"x": bf(np.random.standard_normal((B, HH, WW, C)) * s), "wq": weight(), "bq": bias(),
            "wk": weight(), "bk": bias(), "wv": weight(), "bv": bias()}


def reference(x, wq, bq, wk, bk, wv, bv):
    shifted = np.roll(f64(x), shift=(-SS, -SS), axis=(1, 2))
    win = shifted.reshape(B, GH, WS, GW, WS, C).swapaxes(2, 3).reshape(N * T, C)
    wn = mxq(win, 1, "e4m3")
    q = (wn @ mxq(f64(wq).reshape(C, F), 0, "e4m3")).reshape(N, T, NH, KD) + f64(bq)
    k = (wn @ mxq(f64(wk).reshape(C, F), 0, "e4m3")).reshape(N, T, NH, KD) + f64(bk)
    v = (wn @ mxq(f64(wv).reshape(C, F), 0, "e4m3")).reshape(N, T, NH, KD) + f64(bv)
    return q, k, v

@@ -1,0 +1,170 @@
+from contextlib import ExitStack
+
+import concourse.mybir as mybir
+from concourse.masks import make_identity
+
+F32 = mybir.dt.float32
+BF16 = mybir.dt.bfloat16
+U32 = mybir.dt.uint32
+U8 = mybir.dt.uint8
+FP8X4 = mybir.dt.float8_e4m3fn_x4
+ADD = mybir.AluOpType.add
+
+P = 128
+F = 512
+FLOPS = 2 * 4096 * 512 * 1536
+
+ORDER = [(0, 0), (2, 0), (0, 1), (0, 2), (2, 1), (0, 3), (1, 0), (2, 2), (1, 1), (1, 2), (2, 3), (1, 3)]
+
+
+def tile_windowattentionblock_pa_kernel(tc, x, wq, bq, wk, bk, wv, bv, out_0, out_1, out_2):
+    nc = tc.nc
+    weights = (wq, wk, wv)
+    biases = (bq, bk, bv)
+    x_rows = x.rearrange("b r (cb cl) c -> (b r cb) (cl c)", cl=8)
+    out_blocks = [
+        o.rearrange("(g n) (ti tj) h d -> g (n ti) (tj h d)", g=4, tj=8) for o in (out_0, out_1, out_2)
+    ]
+
+    with ExitStack() as ctx:
+        const = ctx.enter_context(tc.tile_pool(name="const", bufs=1))
+        xq = ctx.enter_context(tc.tile_pool(name="xq", bufs=2))
+        stage = ctx.enter_context(tc.tile_pool(name="stage", bufs=5))
+        psum = ctx.enter_context(tc.psum_pool(name="psum", bufs=1))
+        ctx.enter_context(tc.manual_schedule())
+
+        ident = const.tile([P, P], F32, name="ident")
+        perm_a = const.tile([P, P], F32, name="perm_a")
+        perm_b = const.tile([P, P], F32, name="perm_b")
+        ones = const.tile([P, P], BF16, name="ones")
+        bias_rows = const.tile([P, 3 * F], BF16, name="bias_rows")
+        bias_all = const.tile([P, 3, F], F32, name="bias_all")
+        w_raw = [const.tile([P, 4, F], BF16, name="w_raw%d" % o) for o in range(3)]
+        w_grp = [const.tile([P, F, 4], BF16, name="w_grp%d" % o, align_bytes=64) for o in range(3)]
+        w_codes = [const.tile([P, F], U32, name="w_codes%d" % o, align_bytes=64) for o in range(3)]
+        w_scales = [const.tile([P, F], U8, name="w_scales%d" % o, align_bytes=64) for o in range(3)]
+        x_sb = [const.tile([P, 8 * F], BF16, name="x_sb%d" % g) for g in range(4)]
+
+        def load_w(o):
+            nc.sync.dma_start(
+                out=w_raw[o][:].rearrange("q (u e) f -> q u (e f)", u=2),
+                in_=weights[o].rearrange("(u q e) h d -> q u (e h d)", u=2, e=2),
+            )
+
+        def load_x(blk, c0, c1):
+            r0 = (16 * blk + 4) * 8
+            n = min(P, 512 - r0)
+            nc.sync.dma_start(out=x_sb[blk][0:n, c0:c1], in_=x_rows[r0 : r0 + n, c0:c1])
+            if n < P:
+                nc.sync.dma_start(out=x_sb[blk][n:P, c0:c1], in_=x_rows[0 : P - n, c0:c1])
+
+        nc.vector.memset(bias_rows[:], 0.0)
+        nc.vector.memset(ones[:], 1.0)
+        for o in range(3):
+            nc.scalar.dma_start(
+                out=bias_rows[0:1, o * F : (o + 1) * F], in_=biases[o].rearrange("(o h) d -> o (h d)", o=1)
+            )
+        make_identity(nc, ident[:])
+
+        load_w(0)
+        load_x(0, 4 * F, 8 * F)
+        load_w(2)
+        load_x(0, 0, 4 * F)
+        load_w(1)
+        load_x(1, 0, 8 * F)
+        load_x(2, 0, 8 * F)
+        load_x(3, 0, 8 * F)
+
+        src = ident[:].rearrange("k (a t g) -> k a g t", a=2, t=8, g=8)
+        nc.vector.tensor_copy(out=perm_a[:].rearrange("k (a g t) -> k a g t", a=2, g=8, t=8), in_=src)
+        dst_b = perm_b[:].rearrange("k (a g t) -> k a g t", a=2, g=8, t=8)
+        nc.vector.tensor_copy(out=dst_b[:, :, 0:7, :], in_=src[:, :, 1:8, :])
+        nc.vector.tensor_copy(out=dst_b[:, :, 7:8, :], in_=src[:, :, 0:1, :])
+
+        for o in range(3):
+            bank = psum.tile([P, F], F32, tag="av", bufs=4, name="bank")
+            nc.tensor.matmul(out=bank[:], lhsT=ones[:], rhs=bias_rows[:, o * F : (o + 1) * F], start=True, stop=True)
+            nc.scalar.copy(out=bias_all[:, o, :], in_=bank[:])
+
+        def regroup_w(o):
+            nc.vector.tensor_copy(
+                out=w_grp[o][:].rearrange("p (c i) t -> p c t i", i=4),
+                in_=w_raw[o][:].rearrange("p t (c i) -> p c t i", i=4),
+            )
+
+        def quant_w(o):
+            nc.vector.quantize_mx(
+                out=w_codes[o][:].bitcast(FP8X4),
+                scales=w_scales[o][:],
+                in_=w_grp[o][:].rearrange("p f t -> p (f t)"),
+            )
+
+        def transposes(g):
+            blk, half = divmod(g, 2)
+            perm = perm_a if half == 0 else perm_b
+            words = x_sb[blk][:].bitcast(F32)
+            gx = xq.tile([P, 4 * F], BF16, tag="gx", name="gx", align_bytes=64)
+            gw = gx[:].bitcast(F32)
+            for b in range(2):
+                xt = psum.tile([P, F], F32, tag="xt", bufs=2, name="xt")
+                for s in range(2):
+                    cl = (4 if half == 0 else 0) + 2 * b + s
+                    for u in range(2):
+                        j = 2 * s + u
+                        c0 = cl * 256 + u * P
+                        nc.tensor.transpose(xt[:, j * P : (j + 1) * P], words[:, c0 : c0 + P], perm[:])
+                nc.scalar.copy(
+                    out=gw[:, b * F : (b + 1) * F].rearrange("p (s n u) -> p s n u", s=2, u=2),
+                    in_=xt[:].rearrange("p (s u n) -> p s n u", s=2, u=2),
+                )
+            return gx
+
+        def quant_x(gx):
+            codes = xq.tile([P, F], U32, tag="xc", name="codes", align_bytes=64)
+            scales = xq.tile([P, F], U8, tag="xs", name="scales", align_bytes=64)
+            nc.vector.quantize_mx(out=codes[:].bitcast(FP8X4), scales=scales[:], in_=gx[:])
+            return codes, scales
+
+        regroup_w(0)
+        gx_next = transposes(0)
+        quant_w(0)
+        regroup_w(2)
+        cur = quant_x(gx_next)
+        quant_w(2)
+
+        for g in range(8):
+            blk, half = divmod(g, 2)
+            codes, scales = cur
+            st = [stage.tile([P, 4 * F], F32, tag="st%d" % o, name="st%d" % o) for o in range(3)]
+            for i, (o, s) in enumerate(ORDER):
+                if g == 0 and i == 3:
+                    regroup_w(1)
+                if g == 0 and i == 6:
+                    quant_w(1)
+                if i == 4 and g < 7:
+                    gx_next = transposes(g + 1)
+                if i == 8 and g < 7:
+                    cur = quant_x(gx_next)
+                cols = slice(s * P, (s + 1) * P)
+                dst = st[o][:, s * F : (s + 1) * F]
+                if o == 2:
+                    acc = psum.tile([P, F], F32, tag="as", bufs=2, name="acc_s")
+                else:
+                    acc = psum.tile([P, F], F32, tag="av", bufs=4, name="acc_v")
+                nc.tensor.matmul_mx(
+                    out=acc[:],
+                    lhsT=codes[:, cols].bitcast(FP8X4),
+                    lhsT_scale=scales[:, cols],
+                    rhs=w_codes[o][:].bitcast(FP8X4),
+                    rhs_scale=w_scales[o][:],
+                    start=True,
+                    stop=True,
+                )
+                if o == 2:
+                    nc.scalar.copy(out=dst, in_=acc[:])
+                    nc.gpsimd.tensor_tensor(out=dst, in0=dst, in1=bias_all[:, o, :], op=ADD)
+                else:
+                    nc.vector.tensor_tensor(out=dst, in0=acc[:], in1=bias_all[:, o, :], op=ADD)
+                if s == 3 and o != 2:
+                    nc.sync.dma_start(out=out_blocks[o][blk][:, half * 4 * F : (half + 1) * 4 * F], in_=st[o][:])
+            nc.sync.dma_start(out=out_blocks[2][blk][:, half * 4 * F : (half + 1) * 4 * F], in_=st[2][:])

@@ -14,7 +14,10 @@ P = 128
 F = 512
 FLOPS = 2 * 4096 * 512 * 1536
 
-ORDER = [(0, 0), (2, 0), (0, 1), (0, 2), (2, 1), (0, 3), (1, 0), (2, 2), (1, 1), (1, 2), (2, 3), (1, 3)]
+V_QUADS = [(0, 1), (1, 1)] + [(g, o) for g in range(2, 8) for o in range(2)]
+V_BANKS = [(g, o, s) for (g, o) in V_QUADS for s in range(4)]
+S_BANKS = [(g, 2, s) for g in range(1, 8) for s in range(4)]
+HALF_STORES = [(0, 2), (1, 0)]
 
 
 def tile_windowattentionblock_pa_kernel(tc, x, wq, bq, wk, bk, wv, bv, out_0, out_1, out_2):
@@ -28,7 +31,7 @@ def tile_windowattentionblock_pa_kernel(tc, x, wq, bq, wk, bk, wv, bv, out_0, ou
 
     with ExitStack() as ctx:
         const = ctx.enter_context(tc.tile_pool(name="const", bufs=1))
-        xq = ctx.enter_context(tc.tile_pool(name="xq", bufs=2))
+        xq = ctx.enter_context(tc.tile_pool(name="xq", bufs=3))
         stage = ctx.enter_context(tc.tile_pool(name="stage", bufs=5))
         psum = ctx.enter_context(tc.psum_pool(name="psum", bufs=1))
         ctx.enter_context(tc.manual_schedule())
@@ -38,7 +41,8 @@ def tile_windowattentionblock_pa_kernel(tc, x, wq, bq, wk, bk, wv, bv, out_0, ou
         perm_b = const.tile([P, P], F32, name="perm_b")
         ones = const.tile([P, P], BF16, name="ones")
         bias_rows = const.tile([P, 3 * F], BF16, name="bias_rows")
-        bias_all = const.tile([P, 3, F], F32, name="bias_all")
+        bias_all = const.tile([P, 2, F], F32, name="bias_all")
+        bias_v2 = const.tile([P, 2 * F], F32, name="bias_v2")
         w_raw = [const.tile([P, 4, F], BF16, name="w_raw%d" % o) for o in range(3)]
         w_grp = [const.tile([P, F, 4], BF16, name="w_grp%d" % o, align_bytes=64) for o in range(3)]
         w_codes = [const.tile([P, F], U32, name="w_codes%d" % o, align_bytes=64) for o in range(3)]
@@ -51,6 +55,11 @@ def tile_windowattentionblock_pa_kernel(tc, x, wq, bq, wk, bk, wv, bv, out_0, ou
                 in_=weights[o].rearrange("(u q e) h d -> q u (e h d)", u=2, e=2),
             )
 
+        def load_b(o):
+            nc.sync.dma_start(
+                out=bias_rows[0:1, o * F : (o + 1) * F], in_=biases[o].rearrange("(o h) d -> o (h d)", o=1)
+            )
+
         def load_x(blk, c0, c1):
             r0 = (16 * blk + 4) * 8
             n = min(P, 512 - r0)
@@ -58,18 +67,17 @@ def tile_windowattentionblock_pa_kernel(tc, x, wq, bq, wk, bk, wv, bv, out_0, ou
             if n < P:
                 nc.sync.dma_start(out=x_sb[blk][n:P, c0:c1], in_=x_rows[0 : P - n, c0:c1])
 
-        nc.vector.memset(bias_rows[:], 0.0)
+        nc.vector.memset(bias_rows[:].bitcast(F32), 0.0)
         nc.vector.memset(ones[:], 1.0)
-        for o in range(3):
-            nc.scalar.dma_start(
-                out=bias_rows[0:1, o * F : (o + 1) * F], in_=biases[o].rearrange("(o h) d -> o (h d)", o=1)
-            )
         make_identity(nc, ident[:])
 
-        load_w(0)
         load_x(0, 4 * F, 8 * F)
-        load_w(2)
+        load_b(0)
+        load_w(0)
         load_x(0, 0, 4 * F)
+        load_b(2)
+        load_b(1)
+        load_w(2)
         load_w(1)
         load_x(1, 0, 8 * F)
         load_x(2, 0, 8 * F)
@@ -81,13 +89,17 @@ def tile_windowattentionblock_pa_kernel(tc, x, wq, bq, wk, bk, wv, bv, out_0, ou
         nc.vector.tensor_copy(out=dst_b[:, :, 0:7, :], in_=src[:, :, 1:8, :])
         nc.vector.tensor_copy(out=dst_b[:, :, 7:8, :], in_=src[:, :, 0:1, :])
 
-        for o in range(3):
-            bank = psum.tile([P, F], F32, tag="av", bufs=4, name="bank")
+        def spread_bias(o):
+            bank = psum.tile([P, F], F32, tag="as", bufs=2, name="bank")
             nc.tensor.matmul(out=bank[:], lhsT=ones[:], rhs=bias_rows[:, o * F : (o + 1) * F], start=True, stop=True)
-            nc.scalar.copy(out=bias_all[:, o, :], in_=bank[:])
+            if o == 2:
+                nc.scalar.copy(out=bias_v2[:, 0:F], in_=bank[:])
+                nc.gpsimd.tensor_copy(out=bias_v2[:, F : 2 * F], in_=bias_v2[:, 0:F])
+            else:
+                nc.scalar.copy(out=bias_all[:, o, :], in_=bank[:])
 
-        def regroup_w(o):
-            nc.vector.tensor_copy(
+        def regroup_w(o, engine_copy):
+            engine_copy(
                 out=w_grp[o][:].rearrange("p (c i) t -> p c t i", i=4),
                 in_=w_raw[o][:].rearrange("p t (c i) -> p c t i", i=4),
             )
@@ -99,11 +111,15 @@ def tile_windowattentionblock_pa_kernel(tc, x, wq, bq, wk, bk, wv, bv, out_0, ou
                 in_=w_grp[o][:].rearrange("p f t -> p (f t)"),
             )
 
+        grouped = {}
+        packed = {}
+        staged = {}
+
         def transposes(g):
             blk, half = divmod(g, 2)
             perm = perm_a if half == 0 else perm_b
             words = x_sb[blk][:].bitcast(F32)
-            gx = xq.tile([P, 4 * F], BF16, tag="gx", name="gx", align_bytes=64)
+            gx = xq.tile([P, 4 * F], BF16, tag="gx", bufs=2, name="gx", align_bytes=64)
             gw = gx[:].bitcast(F32)
             for b in range(2):
                 xt = psum.tile([P, F], F32, tag="xt", bufs=2, name="xt")
@@ -117,54 +133,87 @@ def tile_windowattentionblock_pa_kernel(tc, x, wq, bq, wk, bk, wv, bv, out_0, ou
                     out=gw[:, b * F : (b + 1) * F].rearrange("p (s n u) -> p s n u", s=2, u=2),
                     in_=xt[:].rearrange("p (s u n) -> p s n u", s=2, u=2),
                 )
-            return gx
+            grouped[g] = gx
 
-        def quant_x(gx):
+        def quant_x(g):
             codes = xq.tile([P, F], U32, tag="xc", name="codes", align_bytes=64)
             scales = xq.tile([P, F], U8, tag="xs", name="scales", align_bytes=64)
-            nc.vector.quantize_mx(out=codes[:].bitcast(FP8X4), scales=scales[:], in_=gx[:])
-            return codes, scales
+            nc.vector.quantize_mx(out=codes[:].bitcast(FP8X4), scales=scales[:], in_=grouped[g][:])
+            packed[g] = (codes, scales)
 
-        regroup_w(0)
-        gx_next = transposes(0)
-        quant_w(0)
-        regroup_w(2)
-        cur = quant_x(gx_next)
-        quant_w(2)
-
-        for g in range(8):
+        def store(g, o, s0, s1):
             blk, half = divmod(g, 2)
-            codes, scales = cur
-            st = [stage.tile([P, 4 * F], F32, tag="st%d" % o, name="st%d" % o) for o in range(3)]
-            for i, (o, s) in enumerate(ORDER):
-                if g == 0 and i == 3:
-                    regroup_w(1)
-                if g == 0 and i == 6:
-                    quant_w(1)
-                if i == 4 and g < 7:
-                    gx_next = transposes(g + 1)
-                if i == 8 and g < 7:
-                    cur = quant_x(gx_next)
-                cols = slice(s * P, (s + 1) * P)
-                dst = st[o][:, s * F : (s + 1) * F]
-                if o == 2:
-                    acc = psum.tile([P, F], F32, tag="as", bufs=2, name="acc_s")
-                else:
-                    acc = psum.tile([P, F], F32, tag="av", bufs=4, name="acc_v")
-                nc.tensor.matmul_mx(
-                    out=acc[:],
-                    lhsT=codes[:, cols].bitcast(FP8X4),
-                    lhsT_scale=scales[:, cols],
-                    rhs=w_codes[o][:].bitcast(FP8X4),
-                    rhs_scale=w_scales[o][:],
-                    start=True,
-                    stop=True,
-                )
-                if o == 2:
-                    nc.scalar.copy(out=dst, in_=acc[:])
-                    nc.gpsimd.tensor_tensor(out=dst, in0=dst, in1=bias_all[:, o, :], op=ADD)
-                else:
-                    nc.vector.tensor_tensor(out=dst, in0=acc[:], in1=bias_all[:, o, :], op=ADD)
-                if s == 3 and o != 2:
-                    nc.sync.dma_start(out=out_blocks[o][blk][:, half * 4 * F : (half + 1) * 4 * F], in_=st[o][:])
-            nc.sync.dma_start(out=out_blocks[2][blk][:, half * 4 * F : (half + 1) * 4 * F], in_=st[2][:])
+            c0 = half * 4 * F
+            nc.sync.dma_start(
+                out=out_blocks[o][blk][:, c0 + s0 * F : c0 + s1 * F], in_=staged[(g, o)][:, s0 * F : s1 * F]
+            )
+
+        def bank_pass(g, o, s, tag, bufs):
+            if s == 0:
+                staged[(g, o)] = stage.tile([P, 4 * F], F32, tag="st%d" % o, name="st%d" % o)
+            codes, scales = packed[g]
+            cols = slice(s * P, (s + 1) * P)
+            acc = psum.tile([P, F], F32, tag=tag, bufs=bufs, name="acc_" + tag)
+            nc.tensor.matmul_mx(
+                out=acc[:],
+                lhsT=codes[:, cols].bitcast(FP8X4),
+                lhsT_scale=scales[:, cols],
+                rhs=w_codes[o][:].bitcast(FP8X4),
+                rhs_scale=w_scales[o][:],
+                start=True,
+                stop=True,
+            )
+            return acc
+
+        def store_if_full(g, o, s):
+            if (g, o) in HALF_STORES:
+                if s % 2 == 1:
+                    store(g, o, s - 1, s + 1)
+            elif s == 3:
+                store(g, o, 0, 4)
+
+        def vector_bank(g, o, s):
+            acc = bank_pass(g, o, s, "av", 4)
+            bias = bias_v2[:, 0:F] if o == 2 else bias_all[:, o, :]
+            nc.vector.tensor_tensor(out=staged[(g, o)][:, s * F : (s + 1) * F], in0=acc[:], in1=bias, op=ADD)
+            store_if_full(g, o, s)
+
+        def scalar_bank(g, o, s):
+            acc = bank_pass(g, o, s, "as", 2)
+            nc.scalar.copy(out=staged[(g, o)][:, s * F : (s + 1) * F], in_=acc[:])
+            if s % 2 == 1:
+                pair = staged[(g, o)][:, (s - 1) * F : (s + 1) * F]
+                nc.gpsimd.tensor_tensor(out=pair, in0=pair, in1=bias_v2[:], op=ADD)
+                store_if_full(g, o, s)
+
+        transposes(0)
+        regroup_w(0, nc.vector.tensor_copy)
+        quant_w(0)
+        spread_bias(0)
+        transposes(1)
+        quant_x(0)
+        regroup_w(2, nc.scalar.copy)
+        spread_bias(2)
+        for s in range(4):
+            vector_bank(0, 0, s)
+        quant_w(2)
+        scalar_bank(0, 2, 0)
+        scalar_bank(0, 2, 1)
+        quant_x(1)
+        spread_bias(1)
+        regroup_w(1, nc.scalar.copy)
+        for s in range(4):
+            vector_bank(1, 0, s)
+        vector_bank(0, 2, 2)
+        vector_bank(0, 2, 3)
+        quant_w(1)
+
+        for i, bank in enumerate(V_BANKS):
+            g_next = i // 8 + 2
+            if i % 8 == 2 and g_next < 8:
+                transposes(g_next)
+            vector_bank(*bank)
+            if i % 8 == 4 and g_next < 8:
+                quant_x(g_next)
+            if i % 2 == 1:
+                scalar_bank(*S_BANKS[i // 2])

@@ -14,9 +14,6 @@ P = 128
 F = 512
 FLOPS = 2 * 4096 * 512 * 1536
 
-V_QUADS = [(0, 1), (1, 1)] + [(g, o) for g in range(2, 8) for o in range(2)]
-V_BANKS = [(g, o, s) for (g, o) in V_QUADS for s in range(4)]
-S_BANKS = [(g, 2, s) for g in range(1, 8) for s in range(4)]
 HALF_STORES = [(0, 2), (1, 0)]
 
 
@@ -208,12 +205,16 @@ def tile_windowattentionblock_pa_kernel(tc, x, wq, bq, wk, bk, wv, bv, out_0, ou
         vector_bank(0, 2, 3)
         quant_w(1)
 
-        for i, bank in enumerate(V_BANKS):
-            g_next = i // 8 + 2
-            if i % 8 == 2 and g_next < 8:
-                transposes(g_next)
-            vector_bank(*bank)
-            if i % 8 == 4 and g_next < 8:
-                quant_x(g_next)
-            if i % 2 == 1:
-                scalar_bank(*S_BANKS[i // 2])
+        for g in range(1, 8):
+            first = [(0, 1, s) for s in range(4)] if g == 1 else [(g, 0, s) for s in range(4)]
+            banks = first + [(g, 1, s) for s in range(4)] + [(g, 2, 2), (g, 2, 3)]
+            for i, bank in enumerate(banks):
+                if i == 2 and g < 7:
+                    transposes(g + 1)
+                vector_bank(*bank)
+                if i == 1:
+                    scalar_bank(g, 2, 0)
+                if i == 3:
+                    scalar_bank(g, 2, 1)
+                if i == 5 and g < 7:
+                    quant_x(g + 1)

@@ -9,18 +9,17 @@ U32 = mybir.dt.uint32
 U8 = mybir.dt.uint8
 FP8X4 = mybir.dt.float8_e4m3fn_x4
 ADD = mybir.AluOpType.add
+IDENTITY = mybir.ActivationFunctionType.Identity
 
 P = 128
 F = 512
 FLOPS = 2 * 4096 * 512 * 1536
 
-HALF_STORES = [(0, 2), (1, 0)]
-
 
 def tile_windowattentionblock_pa_kernel(tc, x, wq, bq, wk, bk, wv, bv, out_0, out_1, out_2):
     nc = tc.nc
     weights = (wq, wk, wv)
-    biases = (bq, bk, bv)
+    biases = (bq, bk)
     x_rows = x.rearrange("b r (cb cl) c -> (b r cb) (cl c)", cl=8)
     out_blocks = [
         o.rearrange("(g n) (ti tj) h d -> g (n ti) (tj h d)", g=4, tj=8) for o in (out_0, out_1, out_2)
@@ -28,18 +27,21 @@ def tile_windowattentionblock_pa_kernel(tc, x, wq, bq, wk, bk, wv, bv, out_0, ou
 
     with ExitStack() as ctx:
         const = ctx.enter_context(tc.tile_pool(name="const", bufs=1))
-        xq = ctx.enter_context(tc.tile_pool(name="xq", bufs=3))
+        xq = ctx.enter_context(tc.tile_pool(name="xq", bufs=2))
+        flip = ctx.enter_context(tc.tile_pool(name="flip", bufs=2))
         stage = ctx.enter_context(tc.tile_pool(name="stage", bufs=5))
         psum = ctx.enter_context(tc.psum_pool(name="psum", bufs=1))
         ctx.enter_context(tc.manual_schedule())
 
         ident = const.tile([P, P], F32, name="ident")
+        ident_bf = const.tile([P, P], BF16, name="ident_bf")
         perm_a = const.tile([P, P], F32, name="perm_a")
         perm_b = const.tile([P, P], F32, name="perm_b")
         ones = const.tile([P, P], BF16, name="ones")
-        bias_rows = const.tile([P, 3 * F], BF16, name="bias_rows")
+        bias_rows = const.tile([P, 2 * F], BF16, name="bias_rows")
+        bias_v_rows = const.tile([P, P], BF16, name="bias_v_rows")
         bias_all = const.tile([P, 2, F], F32, name="bias_all")
-        bias_v2 = const.tile([P, 2 * F], F32, name="bias_v2")
+        bias_col = const.tile([P, 4], F32, name="bias_col")
         w_raw = [const.tile([P, 4, F], BF16, name="w_raw%d" % o) for o in range(3)]
         w_grp = [const.tile([P, F, 4], BF16, name="w_grp%d" % o, align_bytes=64) for o in range(3)]
         w_codes = [const.tile([P, F], U32, name="w_codes%d" % o, align_bytes=64) for o in range(3)]
@@ -65,17 +67,19 @@ def tile_windowattentionblock_pa_kernel(tc, x, wq, bq, wk, bk, wv, bv, out_0, ou
                 nc.sync.dma_start(out=x_sb[blk][n:P, c0:c1], in_=x_rows[0 : P - n, c0:c1])
 
         nc.vector.memset(bias_rows[:].bitcast(F32), 0.0)
+        nc.vector.memset(bias_v_rows[:].bitcast(F32), 0.0)
         nc.vector.memset(ones[:], 1.0)
         make_identity(nc, ident[:])
+        make_identity(nc, ident_bf[:])
 
         load_x(0, 4 * F, 8 * F)
         load_b(0)
         load_w(0)
-        load_x(0, 0, 4 * F)
-        load_b(2)
-        load_b(1)
         load_w(2)
+        nc.sync.dma_start(out=bias_v_rows[0:4, :], in_=bv.rearrange("(c h) d -> c (h d)", c=4))
+        load_b(1)
         load_w(1)
+        load_x(0, 0, 4 * F)
         load_x(1, 0, 8 * F)
         load_x(2, 0, 8 * F)
         load_x(3, 0, 8 * F)
@@ -87,13 +91,14 @@ def tile_windowattentionblock_pa_kernel(tc, x, wq, bq, wk, bk, wv, bv, out_0, ou
         nc.vector.tensor_copy(out=dst_b[:, :, 7:8, :], in_=src[:, :, 0:1, :])
 
         def spread_bias(o):
-            bank = psum.tile([P, F], F32, tag="as", bufs=2, name="bank")
+            bank = psum.tile([P, F], F32, tag="at", bufs=2, name="bank")
             nc.tensor.matmul(out=bank[:], lhsT=ones[:], rhs=bias_rows[:, o * F : (o + 1) * F], start=True, stop=True)
-            if o == 2:
-                nc.scalar.copy(out=bias_v2[:, 0:F], in_=bank[:])
-                nc.gpsimd.tensor_copy(out=bias_v2[:, F : 2 * F], in_=bias_v2[:, 0:F])
-            else:
-                nc.scalar.copy(out=bias_all[:, o, :], in_=bank[:])
+            nc.scalar.copy(out=bias_all[:, o, :], in_=bank[:])
+
+        def stand_bias_v():
+            bank = psum.tile([P, F], F32, tag="at", bufs=2, name="bank")
+            nc.tensor.matmul(out=bank[:, 0:32], lhsT=bias_v_rows[:], rhs=ident_bf[:, 0:32], start=True, stop=True)
+            nc.scalar.copy(out=bias_col[:], in_=bank[:, 0:4])
 
         def regroup_w(o, engine_copy):
             engine_copy(
@@ -111,15 +116,16 @@ def tile_windowattentionblock_pa_kernel(tc, x, wq, bq, wk, bk, wv, bv, out_0, ou
         grouped = {}
         packed = {}
         staged = {}
+        flipped = {}
 
         def transposes(g):
             blk, half = divmod(g, 2)
             perm = perm_a if half == 0 else perm_b
             words = x_sb[blk][:].bitcast(F32)
-            gx = xq.tile([P, 4 * F], BF16, tag="gx", bufs=2, name="gx", align_bytes=64)
+            gx = xq.tile([P, 4 * F], BF16, tag="gx", name="gx", align_bytes=64)
             gw = gx[:].bitcast(F32)
             for b in range(2):
-                xt = psum.tile([P, F], F32, tag="xt", bufs=2, name="xt")
+                xt = psum.tile([P, F], F32, tag="t", bufs=3, name="xt")
                 for s in range(2):
                     cl = (4 if half == 0 else 0) + 2 * b + s
                     for u in range(2):
@@ -145,12 +151,12 @@ def tile_windowattentionblock_pa_kernel(tc, x, wq, bq, wk, bk, wv, bv, out_0, ou
                 out=out_blocks[o][blk][:, c0 + s0 * F : c0 + s1 * F], in_=staged[(g, o)][:, s0 * F : s1 * F]
             )
 
-        def bank_pass(g, o, s, tag, bufs):
+        def vector_bank(g, o, s):
             if s == 0:
                 staged[(g, o)] = stage.tile([P, 4 * F], F32, tag="st%d" % o, name="st%d" % o)
             codes, scales = packed[g]
             cols = slice(s * P, (s + 1) * P)
-            acc = psum.tile([P, F], F32, tag=tag, bufs=bufs, name="acc_" + tag)
+            acc = psum.tile([P, F], F32, tag="av", bufs=3, name="acc_v")
             nc.tensor.matmul_mx(
                 out=acc[:],
                 lhsT=codes[:, cols].bitcast(FP8X4),
@@ -160,61 +166,75 @@ def tile_windowattentionblock_pa_kernel(tc, x, wq, bq, wk, bk, wv, bv, out_0, ou
                 start=True,
                 stop=True,
             )
-            return acc
-
-        def store_if_full(g, o, s):
-            if (g, o) in HALF_STORES:
-                if s % 2 == 1:
-                    store(g, o, s - 1, s + 1)
-            elif s == 3:
+            nc.vector.tensor_tensor(
+                out=staged[(g, o)][:, s * F : (s + 1) * F], in0=acc[:], in1=bias_all[:, o, :], op=ADD
+            )
+            if s == 3:
                 store(g, o, 0, 4)
 
-        def vector_bank(g, o, s):
-            acc = bank_pass(g, o, s, "av", 4)
-            bias = bias_v2[:, 0:F] if o == 2 else bias_all[:, o, :]
-            nc.vector.tensor_tensor(out=staged[(g, o)][:, s * F : (s + 1) * F], in0=acc[:], in1=bias, op=ADD)
-            store_if_full(g, o, s)
+        def channel_bank(g, c):
+            codes, scales = packed[g]
+            cols = slice(c * P, (c + 1) * P)
+            acc = psum.tile([P, F], F32, tag="at", bufs=2, name="acc_t")
+            nc.tensor.matmul_mx(
+                out=acc[:],
+                lhsT=w_codes[2][:, cols].bitcast(FP8X4),
+                lhsT_scale=w_scales[2][:, cols],
+                rhs=codes[:].bitcast(FP8X4),
+                rhs_scale=scales[:],
+                start=True,
+                stop=True,
+            )
+            vt = flip.tile([P, F], F32, tag="vt%d" % c, name="vt%d" % c)
+            nc.scalar.activation(out=vt[:], in_=acc[:], func=IDENTITY, bias=bias_col[:, c : c + 1], scale=1.0)
+            flipped[(g, c)] = vt
 
-        def scalar_bank(g, o, s):
-            acc = bank_pass(g, o, s, "as", 2)
-            nc.scalar.copy(out=staged[(g, o)][:, s * F : (s + 1) * F], in_=acc[:])
-            if s % 2 == 1:
-                pair = staged[(g, o)][:, (s - 1) * F : (s + 1) * F]
-                nc.gpsimd.tensor_tensor(out=pair, in0=pair, in1=bias_v2[:], op=ADD)
-                store_if_full(g, o, s)
+        def flip_back(g, s, engine_copy):
+            if s == 0:
+                staged[(g, 2)] = stage.tile([P, 4 * F], F32, tag="st2", name="st2")
+            bank = psum.tile([P, F], F32, tag="t", bufs=3, name="bk")
+            for c in range(4):
+                nc.tensor.transpose(bank[:, c * P : (c + 1) * P], flipped[(g, c)][:, s * P : (s + 1) * P], ident[:])
+            engine_copy(out=staged[(g, 2)][:, s * F : (s + 1) * F], in_=bank[:])
 
         transposes(0)
         regroup_w(0, nc.vector.tensor_copy)
         quant_w(0)
         spread_bias(0)
-        transposes(1)
         quant_x(0)
         regroup_w(2, nc.scalar.copy)
-        spread_bias(2)
-        for s in range(4):
-            vector_bank(0, 0, s)
-        quant_w(2)
-        scalar_bank(0, 2, 0)
-        scalar_bank(0, 2, 1)
-        quant_x(1)
-        spread_bias(1)
         regroup_w(1, nc.scalar.copy)
-        for s in range(4):
-            vector_bank(1, 0, s)
-        vector_bank(0, 2, 2)
-        vector_bank(0, 2, 3)
-        quant_w(1)
+        stand_bias_v()
+        spread_bias(1)
 
-        for g in range(1, 8):
-            first = [(0, 1, s) for s in range(4)] if g == 1 else [(g, 0, s) for s in range(4)]
-            banks = first + [(g, 1, s) for s in range(4)] + [(g, 2, 2), (g, 2, 3)]
-            for i, bank in enumerate(banks):
-                if i == 2 and g < 7:
-                    transposes(g + 1)
-                vector_bank(*bank)
-                if i == 1:
-                    scalar_bank(g, 2, 0)
-                if i == 3:
-                    scalar_bank(g, 2, 1)
-                if i == 5 and g < 7:
-                    quant_x(g + 1)
+        for g in range(8):
+            vector_bank(g, 0, 0)
+            vector_bank(g, 0, 1)
+            if g == 0:
+                quant_w(2)
+            channel_bank(g, 0)
+            vector_bank(g, 0, 2)
+            channel_bank(g, 1)
+            vector_bank(g, 0, 3)
+            if g < 7:
+                transposes(g + 1)
+            if g > 0:
+                flip_back(g - 1, 0, nc.scalar.copy)
+            if g == 0:
+                quant_w(1)
+            vector_bank(g, 1, 0)
+            if g < 7:
+                quant_x(g + 1)
+            vector_bank(g, 1, 1)
+            channel_bank(g, 2)
+            vector_bank(g, 1, 2)
+            channel_bank(g, 3)
+            vector_bank(g, 1, 3)
+            if g > 0:
+                for s in range(1, 4):
+                    flip_back(g - 1, s, nc.scalar.copy)
+                store(g - 1, 2, 0, 4)
+        for s in range(4):
+            flip_back(7, s, nc.vector.tensor_copy if s % 2 == 0 else nc.scalar.copy)
+            if s % 2 == 1:
+                store(7, 2, s - 1, s + 1)

@@ -74,9 +74,9 @@ def tile_windowattentionblock_pa_kernel(tc, x, wq, bq, wk, bk, wv, bv, out_0, ou
 
         load_x(0, 4 * F, 8 * F)
         load_b(0)
-        load_w(0)
         load_w(2)
         nc.sync.dma_start(out=bias_v_rows[0:4, :], in_=bv.rearrange("(c h) d -> c (h d)", c=4))
+        load_w(0)
         load_b(1)
         load_w(1)
         load_x(0, 0, 4 * F)
@@ -125,7 +125,7 @@ def tile_windowattentionblock_pa_kernel(tc, x, wq, bq, wk, bk, wv, bv, out_0, ou
             gx = xq.tile([P, 4 * F], BF16, tag="gx", name="gx", align_bytes=64)
             gw = gx[:].bitcast(F32)
             for b in range(2):
-                xt = psum.tile([P, F], F32, tag="t", bufs=3, name="xt")
+                xt = psum.tile([P, F], F32, tag="t", bufs=2, name="xt")
                 for s in range(2):
                     cl = (4 if half == 0 else 0) + 2 * b + s
                     for u in range(2):
@@ -156,7 +156,7 @@ def tile_windowattentionblock_pa_kernel(tc, x, wq, bq, wk, bk, wv, bv, out_0, ou
                 staged[(g, o)] = stage.tile([P, 4 * F], F32, tag="st%d" % o, name="st%d" % o)
             codes, scales = packed[g]
             cols = slice(s * P, (s + 1) * P)
-            acc = psum.tile([P, F], F32, tag="av", bufs=3, name="acc_v")
+            acc = psum.tile([P, F], F32, tag="av", bufs=4, name="acc_v")
             nc.tensor.matmul_mx(
                 out=acc[:],
                 lhsT=codes[:, cols].bitcast(FP8X4),
@@ -169,7 +169,9 @@ def tile_windowattentionblock_pa_kernel(tc, x, wq, bq, wk, bk, wv, bv, out_0, ou
             nc.vector.tensor_tensor(
                 out=staged[(g, o)][:, s * F : (s + 1) * F], in0=acc[:], in1=bias_all[:, o, :], op=ADD
             )
-            if s == 3:
+            if g == 7 and s % 2 == 1:
+                store(g, o, s - 1, s + 1)
+            elif s == 3:
                 store(g, o, 0, 4)
 
         def channel_bank(g, c):
@@ -192,49 +194,46 @@ def tile_windowattentionblock_pa_kernel(tc, x, wq, bq, wk, bk, wv, bv, out_0, ou
         def flip_back(g, s, engine_copy):
             if s == 0:
                 staged[(g, 2)] = stage.tile([P, 4 * F], F32, tag="st2", name="st2")
-            bank = psum.tile([P, F], F32, tag="t", bufs=3, name="bk")
+            bank = psum.tile([P, F], F32, tag="t", bufs=2, name="bk")
             for c in range(4):
                 nc.tensor.transpose(bank[:, c * P : (c + 1) * P], flipped[(g, c)][:, s * P : (s + 1) * P], ident[:])
             engine_copy(out=staged[(g, 2)][:, s * F : (s + 1) * F], in_=bank[:])
+            if s % 2 == 1:
+                store(g, 2, s - 1, s + 1)
 
         transposes(0)
+        regroup_w(2, nc.scalar.copy)
+        quant_x(0)
         regroup_w(0, nc.vector.tensor_copy)
         quant_w(0)
         spread_bias(0)
-        quant_x(0)
-        regroup_w(2, nc.scalar.copy)
-        regroup_w(1, nc.scalar.copy)
         stand_bias_v()
-        spread_bias(1)
+        quant_w(2)
 
         for g in range(8):
             vector_bank(g, 0, 0)
             vector_bank(g, 0, 1)
-            if g == 0:
-                quant_w(2)
             channel_bank(g, 0)
-            vector_bank(g, 0, 2)
             channel_bank(g, 1)
-            vector_bank(g, 0, 3)
             if g < 7:
                 transposes(g + 1)
-            if g > 0:
-                flip_back(g - 1, 0, nc.scalar.copy)
+            vector_bank(g, 0, 2)
+            vector_bank(g, 0, 3)
+            channel_bank(g, 2)
+            channel_bank(g, 3)
             if g == 0:
+                spread_bias(1)
+                regroup_w(1, nc.vector.tensor_copy)
                 quant_w(1)
+            else:
+                flip_back(g - 1, 2, nc.scalar.copy)
+                flip_back(g - 1, 3, nc.scalar.copy)
             vector_bank(g, 1, 0)
             if g < 7:
                 quant_x(g + 1)
-            vector_bank(g, 1, 1)
-            channel_bank(g, 2)
-            vector_bank(g, 1, 2)
-            channel_bank(g, 3)
-            vector_bank(g, 1, 3)
-            if g > 0:
-                for s in range(1, 4):
-                    flip_back(g - 1, s, nc.scalar.copy)
-                store(g - 1, 2, 0, 4)
-        for s in range(4):
-            flip_back(7, s, nc.vector.tensor_copy if s % 2 == 0 else nc.scalar.copy)
-            if s % 2 == 1:
-                store(7, 2, s - 1, s + 1)
+            for s in range(1, 4):
+                vector_bank(g, 1, s)
+            flip_back(g, 0, nc.scalar.copy)
+            flip_back(g, 1, nc.scalar.copy)
+        flip_back(7, 2, nc.vector.tensor_copy)
+        flip_back(7, 3, nc.scalar.copy)

@@ -72,11 +72,12 @@ def tile_windowattentionblock_pa_kernel(tc, x, wq, bq, wk, bk, wv, bv, out_0, ou
         make_identity(nc, ident[:])
         make_identity(nc, ident_bf[:])
 
-        load_x(0, 4 * F, 8 * F)
+        load_x(0, 4 * F, 6 * F)
         load_b(0)
+        load_w(0)
+        load_x(0, 6 * F, 8 * F)
         load_w(2)
         nc.sync.dma_start(out=bias_v_rows[0:4, :], in_=bv.rearrange("(c h) d -> c (h d)", c=4))
-        load_w(0)
         load_b(1)
         load_w(1)
         load_x(0, 0, 4 * F)
@@ -125,7 +126,7 @@ def tile_windowattentionblock_pa_kernel(tc, x, wq, bq, wk, bk, wv, bv, out_0, ou
             gx = xq.tile([P, 4 * F], BF16, tag="gx", name="gx", align_bytes=64)
             gw = gx[:].bitcast(F32)
             for b in range(2):
-                xt = psum.tile([P, F], F32, tag="t", bufs=2, name="xt")
+                xt = psum.tile([P, F], F32, tag="t", bufs=3, name="xt")
                 for s in range(2):
                     cl = (4 if half == 0 else 0) + 2 * b + s
                     for u in range(2):
@@ -156,7 +157,7 @@ def tile_windowattentionblock_pa_kernel(tc, x, wq, bq, wk, bk, wv, bv, out_0, ou
                 staged[(g, o)] = stage.tile([P, 4 * F], F32, tag="st%d" % o, name="st%d" % o)
             codes, scales = packed[g]
             cols = slice(s * P, (s + 1) * P)
-            acc = psum.tile([P, F], F32, tag="av", bufs=4, name="acc_v")
+            acc = psum.tile([P, F], F32, tag="av", bufs=3, name="acc_v")
             nc.tensor.matmul_mx(
                 out=acc[:],
                 lhsT=codes[:, cols].bitcast(FP8X4),
@@ -194,46 +195,49 @@ def tile_windowattentionblock_pa_kernel(tc, x, wq, bq, wk, bk, wv, bv, out_0, ou
         def flip_back(g, s, engine_copy):
             if s == 0:
                 staged[(g, 2)] = stage.tile([P, 4 * F], F32, tag="st2", name="st2")
-            bank = psum.tile([P, F], F32, tag="t", bufs=2, name="bk")
+            bank = psum.tile([P, F], F32, tag="t", bufs=3, name="bk")
             for c in range(4):
                 nc.tensor.transpose(bank[:, c * P : (c + 1) * P], flipped[(g, c)][:, s * P : (s + 1) * P], ident[:])
             engine_copy(out=staged[(g, 2)][:, s * F : (s + 1) * F], in_=bank[:])
-            if s % 2 == 1:
-                store(g, 2, s - 1, s + 1)
 
         transposes(0)
-        regroup_w(2, nc.scalar.copy)
-        quant_x(0)
         regroup_w(0, nc.vector.tensor_copy)
         quant_w(0)
         spread_bias(0)
+        quant_x(0)
+        regroup_w(2, nc.scalar.copy)
         stand_bias_v()
-        quant_w(2)
 
         for g in range(8):
+            if g > 0:
+                for s in range(3):
+                    flip_back(g - 1, s, nc.scalar.copy)
             vector_bank(g, 0, 0)
             vector_bank(g, 0, 1)
+            if g == 0:
+                quant_w(2)
             channel_bank(g, 0)
+            vector_bank(g, 0, 2)
             channel_bank(g, 1)
+            vector_bank(g, 0, 3)
+            if g > 0:
+                flip_back(g - 1, 3, nc.scalar.copy)
+                store(g - 1, 2, 0, 4)
             if g < 7:
                 transposes(g + 1)
-            vector_bank(g, 0, 2)
-            vector_bank(g, 0, 3)
-            channel_bank(g, 2)
-            channel_bank(g, 3)
             if g == 0:
                 spread_bias(1)
                 regroup_w(1, nc.vector.tensor_copy)
                 quant_w(1)
-            else:
-                flip_back(g - 1, 2, nc.scalar.copy)
-                flip_back(g - 1, 3, nc.scalar.copy)
             vector_bank(g, 1, 0)
             if g < 7:
                 quant_x(g + 1)
-            for s in range(1, 4):
-                vector_bank(g, 1, s)
-            flip_back(g, 0, nc.scalar.copy)
-            flip_back(g, 1, nc.scalar.copy)
-        flip_back(7, 2, nc.vector.tensor_copy)
-        flip_back(7, 3, nc.scalar.copy)
+            vector_bank(g, 1, 1)
+            channel_bank(g, 2)
+            vector_bank(g, 1, 2)
+            channel_bank(g, 3)
+            vector_bank(g, 1, 3)
+        for s in range(4):
+            flip_back(7, s, nc.vector.tensor_copy if s % 2 == 0 else nc.scalar.copy)
+            if s % 2 == 1:
+                store(7, 2, s - 1, s + 1)

@@ -31,7 +31,6 @@ def tile_windowattentionblock_pa_kernel(tc, x, wq, bq, wk, bk, wv, bv, out_0, ou
         flip = ctx.enter_context(tc.tile_pool(name="flip", bufs=2))
         stage = ctx.enter_context(tc.tile_pool(name="stage", bufs=5))
         psum = ctx.enter_context(tc.psum_pool(name="psum", bufs=1))
-        ctx.enter_context(tc.manual_schedule())
 
         ident = const.tile([P, P], F32, name="ident")
         ident_bf = const.tile([P, P], BF16, name="ident_bf")
@@ -72,10 +71,9 @@ def tile_windowattentionblock_pa_kernel(tc, x, wq, bq, wk, bk, wv, bv, out_0, ou
         make_identity(nc, ident[:])
         make_identity(nc, ident_bf[:])
 
-        load_x(0, 4 * F, 6 * F)
+        load_x(0, 4 * F, 8 * F)
         load_b(0)
         load_w(0)
-        load_x(0, 6 * F, 8 * F)
         load_w(2)
         nc.sync.dma_start(out=bias_v_rows[0:4, :], in_=bv.rearrange("(c h) d -> c (h d)", c=4))
         load_b(1)
@@ -170,9 +168,7 @@ def tile_windowattentionblock_pa_kernel(tc, x, wq, bq, wk, bk, wv, bv, out_0, ou
             nc.vector.tensor_tensor(
                 out=staged[(g, o)][:, s * F : (s + 1) * F], in0=acc[:], in1=bias_all[:, o, :], op=ADD
             )
-            if g == 7 and s % 2 == 1:
-                store(g, o, s - 1, s + 1)
-            elif s == 3:
+            if s == 3:
                 store(g, o, 0, 4)
 
         def channel_bank(g, c):
@@ -206,12 +202,11 @@ def tile_windowattentionblock_pa_kernel(tc, x, wq, bq, wk, bk, wv, bv, out_0, ou
         spread_bias(0)
         quant_x(0)
         regroup_w(2, nc.scalar.copy)
+        regroup_w(1, nc.scalar.copy)
         stand_bias_v()
+        spread_bias(1)
 
         for g in range(8):
-            if g > 0:
-                for s in range(3):
-                    flip_back(g - 1, s, nc.scalar.copy)
             vector_bank(g, 0, 0)
             vector_bank(g, 0, 1)
             if g == 0:
@@ -220,14 +215,11 @@ def tile_windowattentionblock_pa_kernel(tc, x, wq, bq, wk, bk, wv, bv, out_0, ou
             vector_bank(g, 0, 2)
             channel_bank(g, 1)
             vector_bank(g, 0, 3)
-            if g > 0:
-                flip_back(g - 1, 3, nc.scalar.copy)
-                store(g - 1, 2, 0, 4)
             if g < 7:
                 transposes(g + 1)
+            if g > 0:
+                flip_back(g - 1, 0, nc.scalar.copy)
             if g == 0:
-                spread_bias(1)
-                regroup_w(1, nc.vector.tensor_copy)
                 quant_w(1)
             vector_bank(g, 1, 0)
             if g < 7:
@@ -237,6 +229,10 @@ def tile_windowattentionblock_pa_kernel(tc, x, wq, bq, wk, bk, wv, bv, out_0, ou
             vector_bank(g, 1, 2)
             channel_bank(g, 3)
             vector_bank(g, 1, 3)
+            if g > 0:
+                for s in range(1, 4):
+                    flip_back(g - 1, s, nc.scalar.copy)
+                store(g - 1, 2, 0, 4)
         for s in range(4):
             flip_back(7, s, nc.vector.tensor_copy if s % 2 == 0 else nc.scalar.copy)
             if s % 2 == 1:

from contextlib import ExitStack

import concourse.mybir as mybir
from concourse.masks import make_identity

F32 = mybir.dt.float32
BF16 = mybir.dt.bfloat16
U32 = mybir.dt.uint32
U8 = mybir.dt.uint8
FP8X4 = mybir.dt.float8_e4m3fn_x4
ADD = mybir.AluOpType.add
IDENTITY = mybir.ActivationFunctionType.Identity

P = 128
F = 512
FLOPS = 2 * 4096 * 512 * 1536


def tile_windowattentionblock_pa_kernel(tc, x, wq, bq, wk, bk, wv, bv, out_0, out_1, out_2):
    nc = tc.nc
    weights = (wq, wk, wv)
    biases = (bq, bk)
    x_rows = x.rearrange("b r (cb cl) c -> (b r cb) (cl c)", cl=8)
    out_blocks = [
        o.rearrange("(g n) (ti tj) h d -> g (n ti) (tj h d)", g=4, tj=8) for o in (out_0, out_1, out_2)
    ]

    with ExitStack() as ctx:
        const = ctx.enter_context(tc.tile_pool(name="const", bufs=1))
        xq = ctx.enter_context(tc.tile_pool(name="xq", bufs=2))
        flip = ctx.enter_context(tc.tile_pool(name="flip", bufs=2))
        stage = ctx.enter_context(tc.tile_pool(name="stage", bufs=5))
        psum = ctx.enter_context(tc.psum_pool(name="psum", bufs=1))

        ident = const.tile([P, P], F32, name="ident")
        ident_bf = const.tile([P, P], BF16, name="ident_bf")
        perm_a = const.tile([P, P], F32, name="perm_a")
        perm_b = const.tile([P, P], F32, name="perm_b")
        ones = const.tile([P, P], BF16, name="ones")
        bias_rows = const.tile([P, 2 * F], BF16, name="bias_rows")
        bias_v_rows = const.tile([P, P], BF16, name="bias_v_rows")
        bias_all = const.tile([P, 2, F], F32, name="bias_all")
        bias_col = const.tile([P, 4], F32, name="bias_col")
        w_raw = [const.tile([P, 4, F], BF16, name="w_raw%d" % o) for o in range(3)]
        w_grp = [const.tile([P, F, 4], BF16, name="w_grp%d" % o, align_bytes=64) for o in range(3)]
        w_codes = [const.tile([P, F], U32, name="w_codes%d" % o, align_bytes=64) for o in range(3)]
        w_scales = [const.tile([P, F], U8, name="w_scales%d" % o, align_bytes=64) for o in range(3)]
        x_sb = [const.tile([P, 8 * F], BF16, name="x_sb%d" % g) for g in range(4)]

        def load_w(o):
            nc.sync.dma_start(
                out=w_raw[o][:].rearrange("q (u e) f -> q u (e f)", u=2),
                in_=weights[o].rearrange("(u q e) h d -> q u (e h d)", u=2, e=2),
            )

        def load_b(o):
            nc.sync.dma_start(
                out=bias_rows[0:1, o * F : (o + 1) * F], in_=biases[o].rearrange("(o h) d -> o (h d)", o=1)
            )

        def load_x(blk, c0, c1):
            r0 = (16 * blk + 4) * 8
            n = min(P, 512 - r0)
            nc.sync.dma_start(out=x_sb[blk][0:n, c0:c1], in_=x_rows[r0 : r0 + n, c0:c1])
            if n < P:
                nc.sync.dma_start(out=x_sb[blk][n:P, c0:c1], in_=x_rows[0 : P - n, c0:c1])

        nc.vector.memset(bias_rows[:].bitcast(F32), 0.0)
        nc.vector.memset(bias_v_rows[:].bitcast(F32), 0.0)
        nc.vector.memset(ones[:], 1.0)
        make_identity(nc, ident[:])
        make_identity(nc, ident_bf[:])

        load_x(0, 4 * F, 8 * F)
        load_b(0)
        load_w(0)
        load_w(2)
        nc.sync.dma_start(out=bias_v_rows[0:4, :], in_=bv.rearrange("(c h) d -> c (h d)", c=4))
        load_b(1)
        load_w(1)
        load_x(0, 0, 4 * F)
        load_x(1, 0, 8 * F)
        load_x(2, 0, 8 * F)
        load_x(3, 0, 8 * F)

        src = ident[:].rearrange("k (a t g) -> k a g t", a=2, t=8, g=8)
        nc.vector.tensor_copy(out=perm_a[:].rearrange("k (a g t) -> k a g t", a=2, g=8, t=8), in_=src)
        dst_b = perm_b[:].rearrange("k (a g t) -> k a g t", a=2, g=8, t=8)
        nc.vector.tensor_copy(out=dst_b[:, :, 0:7, :], in_=src[:, :, 1:8, :])
        nc.vector.tensor_copy(out=dst_b[:, :, 7:8, :], in_=src[:, :, 0:1, :])

        def spread_bias(o):
            bank = psum.tile([P, F], F32, tag="at", bufs=2, name="bank")
            nc.tensor.matmul(out=bank[:], lhsT=ones[:], rhs=bias_rows[:, o * F : (o + 1) * F], start=True, stop=True)
            nc.scalar.copy(out=bias_all[:, o, :], in_=bank[:])

        def stand_bias_v():
            bank = psum.tile([P, F], F32, tag="at", bufs=2, name="bank")
            nc.tensor.matmul(out=bank[:, 0:32], lhsT=bias_v_rows[:], rhs=ident_bf[:, 0:32], start=True, stop=True)
            nc.scalar.copy(out=bias_col[:], in_=bank[:, 0:4])

        def regroup_w(o, engine_copy):
            engine_copy(
                out=w_grp[o][:].rearrange("p (c i) t -> p c t i", i=4),
                in_=w_raw[o][:].rearrange("p t (c i) -> p c t i", i=4),
            )

        def quant_w(o):
            nc.vector.quantize_mx(
                out=w_codes[o][:].bitcast(FP8X4),
                scales=w_scales[o][:],
                in_=w_grp[o][:].rearrange("p f t -> p (f t)"),
            )

        grouped = {}
        packed = {}
        staged = {}
        flipped = {}

        def transposes(g):
            blk, half = divmod(g, 2)
            perm = perm_a if half == 0 else perm_b
            words = x_sb[blk][:].bitcast(F32)
            gx = xq.tile([P, 4 * F], BF16, tag="gx", name="gx", align_bytes=64)
            gw = gx[:].bitcast(F32)
            for b in range(2):
                xt = psum.tile([P, F], F32, tag="t", bufs=3, name="xt")
                for s in range(2):
                    cl = (4 if half == 0 else 0) + 2 * b + s
                    for u in range(2):
                        j = 2 * s + u
                        c0 = cl * 256 + u * P
                        nc.tensor.transpose(xt[:, j * P : (j + 1) * P], words[:, c0 : c0 + P], perm[:])
                nc.scalar.copy(
                    out=gw[:, b * F : (b + 1) * F].rearrange("p (s n u) -> p s n u", s=2, u=2),
                    in_=xt[:].rearrange("p (s u n) -> p s n u", s=2, u=2),
                )
            grouped[g] = gx

        def quant_x(g):
            codes = xq.tile([P, F], U32, tag="xc", name="codes", align_bytes=64)
            scales = xq.tile([P, F], U8, tag="xs", name="scales", align_bytes=64)
            nc.vector.quantize_mx(out=codes[:].bitcast(FP8X4), scales=scales[:], in_=grouped[g][:])
            packed[g] = (codes, scales)

        def store(g, o, s0, s1):
            blk, half = divmod(g, 2)
            c0 = half * 4 * F
            nc.sync.dma_start(
                out=out_blocks[o][blk][:, c0 + s0 * F : c0 + s1 * F], in_=staged[(g, o)][:, s0 * F : s1 * F]
            )

        def vector_bank(g, o, s):
            if s == 0:
                staged[(g, o)] = stage.tile([P, 4 * F], F32, tag="st%d" % o, name="st%d" % o)
            codes, scales = packed[g]
            cols = slice(s * P, (s + 1) * P)
            acc = psum.tile([P, F], F32, tag="av", bufs=3, name="acc_v")
            nc.tensor.matmul_mx(
                out=acc[:],
                lhsT=codes[:, cols].bitcast(FP8X4),
                lhsT_scale=scales[:, cols],
                rhs=w_codes[o][:].bitcast(FP8X4),
                rhs_scale=w_scales[o][:],
                start=True,
                stop=True,
            )
            nc.vector.tensor_tensor(
                out=staged[(g, o)][:, s * F : (s + 1) * F], in0=acc[:], in1=bias_all[:, o, :], op=ADD
            )
            if s == 3:
                store(g, o, 0, 4)

        def channel_bank(g, c):
            codes, scales = packed[g]
            cols = slice(c * P, (c + 1) * P)
            acc = psum.tile([P, F], F32, tag="at", bufs=2, name="acc_t")
            nc.tensor.matmul_mx(
                out=acc[:],
                lhsT=w_codes[2][:, cols].bitcast(FP8X4),
                lhsT_scale=w_scales[2][:, cols],
                rhs=codes[:].bitcast(FP8X4),
                rhs_scale=scales[:],
                start=True,
                stop=True,
            )
            vt = flip.tile([P, F], F32, tag="vt%d" % c, name="vt%d" % c)
            nc.scalar.activation(out=vt[:], in_=acc[:], func=IDENTITY, bias=bias_col[:, c : c + 1], scale=1.0)
            flipped[(g, c)] = vt

        def flip_back(g, s, engine_copy):
            if s == 0:
                staged[(g, 2)] = stage.tile([P, 4 * F], F32, tag="st2", name="st2")
            bank = psum.tile([P, F], F32, tag="t", bufs=3, name="bk")
            for c in range(4):
                nc.tensor.transpose(bank[:, c * P : (c + 1) * P], flipped[(g, c)][:, s * P : (s + 1) * P], ident[:])
            engine_copy(out=staged[(g, 2)][:, s * F : (s + 1) * F], in_=bank[:])

        transposes(0)
        regroup_w(0, nc.vector.tensor_copy)
        quant_w(0)
        spread_bias(0)
        quant_x(0)
        regroup_w(2, nc.scalar.copy)
        regroup_w(1, nc.scalar.copy)
        stand_bias_v()
        spread_bias(1)

        for g in range(8):
            vector_bank(g, 0, 0)
            vector_bank(g, 0, 1)
            if g == 0:
                quant_w(2)
            channel_bank(g, 0)
            vector_bank(g, 0, 2)
            channel_bank(g, 1)
            vector_bank(g, 0, 3)
            if g < 7:
                transposes(g + 1)
            if g > 0:
                flip_back(g - 1, 0, nc.scalar.copy)
            if g == 0:
                quant_w(1)
            vector_bank(g, 1, 0)
            if g < 7:
                quant_x(g + 1)
            vector_bank(g, 1, 1)
            channel_bank(g, 2)
            vector_bank(g, 1, 2)
            channel_bank(g, 3)
            vector_bank(g, 1, 3)
            if g > 0:
                for s in range(1, 4):
                    flip_back(g - 1, s, nc.scalar.copy)
                store(g - 1, 2, 0, 4)
        for s in range(4):
            flip_back(7, s, nc.vector.tensor_copy if s % 2 == 0 else nc.scalar.copy)
            if s % 2 == 1:
                store(7, 2, s - 1, s + 1)
